import numpy as np
import ml_dtypes


def mxq(x, axis, fmt="e4m3"):
    dtype, down = {"e4m3": (ml_dtypes.float8_e4m3fn, 7), "e5m2": (ml_dtypes.float8_e5m2, 14)}[fmt]
    v = np.moveaxis(np.asarray(x, np.float32).astype(ml_dtypes.bfloat16).astype(np.float64), axis, -1)
    blocks = v.reshape(v.shape[:-1] + (-1, 32))
    amax = np.abs(blocks).max(-1, keepdims=True)
    byte = np.maximum(np.where(amax > 0, np.frexp(amax)[1] - 1 + 127, 0) - down, 1)
    scale = np.exp2(byte - 127.0)
    codes = (blocks / scale).astype(np.float32).astype(dtype).astype(np.float64)
    return np.moveaxis((codes * scale).reshape(v.shape), -1, axis)


WIDE = False


def mx_kscale(k):
    if not WIDE:
        return np.ones(k)
    levels = np.array([10, -10, 5, -5, 0])
    if k % 512:
        return np.exp2(np.random.permutation(np.resize(levels, k // 32))).repeat(32)
    a = np.empty((k // 512, 16))
    for p in range(k // 512):
        a[p, :8] = np.random.permutation(np.resize(levels, 8))
        for g in range(8):
            far = levels[np.abs(levels - a[p, g]) >= 10]
            a[p, g + 8] = far[np.random.randint(len(far))]
    return np.exp2(a.ravel()).repeat(32)


BF16 = ml_dtypes.bfloat16


def bf(x):
    return np.asarray(x, np.float32).astype(BF16)


def f64(x):
    return np.asarray(x).astype(np.float64)


B, D, ELL = 4096, 512, 4


def draw0():
    s, t = mx_kscale(D), mx_kscale(D)
    return {"x": bf(np.random.standard_normal((B, D))),
            "phi_j": bf(np.random.standard_normal((B, D)) * 0.7 * t / s),
            "phi_k": bf(np.random.standard_normal((B, D)) * 0.7 * s),
            "w_i": bf(np.random.standard_normal((D, D)) / np.sqrt(D) / t),
            "w_j": bf(np.random.standard_normal((D, D)) / np.sqrt(D) * t[:, None] / s)}


def core(x, phi_j, phi_k, w_i, w_j):
    x, phi_j, phi_k = f64(x), f64(phi_j), f64(phi_k)
    th = np.tanh(x)
    d1 = 1.0 - th * th
    d2 = -2.0 * th * d1
    jvp_jk = mxq(d1 * phi_k, 1, "e4m3") @ mxq(f64(w_j), 1, "e4m3").T
    u = d2 * phi_k * phi_j + d1 * jvp_jk
    return mxq(u, 1, "e4m3") @ mxq(f64(w_i), 1, "e4m3").T


def e4m3fn_bytes(y):
    return np.clip(np.asarray(y, np.float64), -448.0, 448.0).astype(np.float32).astype(ml_dtypes.float8_e4m3fn).view(np.uint8)


def e4m3fn_values(b):
    return np.asarray(b, np.uint8).view(ml_dtypes.float8_e4m3fn).astype(np.float64)


def setup_inputs():
    d = draw0()
    x0 = np.asarray(d['w_i']).astype(np.float64)
    s = (np.max(np.abs(x0), axis=(0,), keepdims=True) / 448.0).astype(np.float32)
    out = {}
    for k, v in d.items():
        if k == 'w_i':
            out['w_i_bytes'] = e4m3fn_bytes(x0 / s.astype(np.float64))
            out['w_i_scale'] = s
        else:
            out[k] = v
    return out


def reference(x, phi_j, phi_k, w_i_bytes, w_i_scale, w_j):
    return core(x, phi_j, phi_k, e4m3fn_values(w_i_bytes) * w_i_scale.astype(np.float64), w_j)

@@ -1,0 +1,320 @@
+from contextlib import ExitStack
+
+import concourse.mybir as mybir
+from concourse.masks import make_identity
+
+TOKENS, D = 4096, 512
+P = 128
+PACK = 4
+SUB = 2
+N = P * SUB
+MACROS = TOKENS // N
+
+FLOPS = 2 * 2 * TOKENS * D * D
+
+F32 = mybir.dt.float32
+BF16 = mybir.dt.bfloat16
+U32 = mybir.dt.uint32
+U8 = mybir.dt.uint8
+FP8 = mybir.dt.float8_e4m3fn
+FP8X4 = mybir.dt.float8_e4m3fn_x4
+ACT = mybir.ActivationFunctionType
+ALU = mybir.AluOpType
+
+
+def tile_inimnetdisc_pa_t_kernel(tc, x, phi_j, phi_k, w_i_bytes, w_i_scale, w_j, out):
+    nc = tc.nc
+    x_h = x.rearrange("(m r s) d -> m r s d", r=P, s=SUB)
+    j_h = phi_j.rearrange("(m r s) d -> m r s d", r=P, s=SUB)
+    k_h = phi_k.rearrange("(m r s) d -> m r s d", r=P, s=SUB)
+    o_h = out.rearrange("(m r s) d -> m r s d", r=P, s=SUB)
+
+    with ExitStack() as ctx:
+        keep = ctx.enter_context(tc.tile_pool(name="keep", bufs=1))
+        loads = ctx.enter_context(tc.tile_pool(name="loads", bufs=6))
+        work = ctx.enter_context(tc.tile_pool(name="work", bufs=3))
+        psum = ctx.enter_context(tc.psum_pool(name="psum", bufs=1))
+        ctx.enter_context(tc.manual_schedule())
+
+        ident = keep.tile([P, P], F32, name="ident")
+        minus_one = keep.tile([P, 1], F32, name="minus_one")
+        warm = keep.tile([P, 1], F32, name="warm")
+        wj_raw = keep.tile([P, PACK, D], BF16, name="wj_raw")
+        wi_byte = keep.tile([P, PACK, D], U8, name="wi_byte")
+        wi_val = keep.tile([P, PACK, D], BF16, name="wi_val")
+        wi_sc = keep.tile([P, PACK], F32, name="wi_sc")
+        wj_grp = keep.tile([P, D, PACK], BF16, name="wj_grp", align_bytes=64)
+        wi_grp = keep.tile([P, D, PACK], BF16, name="wi_grp", align_bytes=64)
+        wj_codes = keep.tile([P, D], U32, name="wj_codes", align_bytes=64)
+        wj_scales = keep.tile([P, D], U8, name="wj_scales", align_bytes=64)
+        wi_codes = keep.tile([P, D], U32, name="wi_codes", align_bytes=64)
+        wi_scales = keep.tile([P, D], U8, name="wi_scales", align_bytes=64)
+
+        xs, js, ks, ps = {}, {}, {}, {}
+        ts, ds, gs, qs, ws, us = {}, {}, {}, {}, {}, {}
+        t2s, gq, uq, outs = {}, {}, {}, {}
+        xb, kb, pb, vb, ob = {}, {}, {}, {}, {}
+
+        def load_x(m):
+            xs[m] = loads.tile([P, SUB, D], BF16, name="x_in")
+            nc.sync.dma_start(out=xs[m][:], in_=x_h[m])
+
+        def load_k(m):
+            ks[m] = loads.tile([P, SUB, D], BF16, name="k_in")
+            nc.sync.dma_start(out=ks[m][:], in_=k_h[m])
+
+        def load_j(m):
+            js[m] = loads.tile([P, SUB, D], BF16, name="j_in")
+            nc.sync.dma_start(out=js[m][:], in_=j_h[m])
+
+        def load(m):
+            if m < MACROS:
+                load_x(m)
+                load_k(m)
+                load_j(m)
+
+        def turn(src, bank):
+            words = src[:].rearrange("r s d -> r (s d)").bitcast(F32).rearrange("r (s w) -> r s w", s=SUB)
+            for u in range(2):
+                for s in range(SUB):
+                    nc.tensor.transpose(bank[:, u, s, :], words[:, s, u : D // 2 : 2], ident[:])
+
+        def turn_x(m):
+            xb[m] = psum.tile([P, 2, SUB, P], F32, name="bank_x")
+            turn(xs[m], xb[m])
+
+        def turn_k(m):
+            kb[m] = psum.tile([P, 2, SUB, P], F32, name="bank_k")
+            turn(ks[m], kb[m])
+
+        def pairs(bank):
+            return bank[:].rearrange("p u s r -> p (u s r)").bitcast(BF16).rearrange("p (u n e) -> p n u e", u=2, e=2)
+
+        def split(tile):
+            return tile[:].rearrange("p n (u e) -> p n u e", u=2)
+
+        def tanh(m):
+            ts[m] = work.tile([P, N, PACK], F32, name="t")
+            nc.scalar.activation(out=split(ts[m]), in_=pairs(xb[m]), func=ACT.Tanh)
+
+        def square(m):
+            t2s[m] = work.tile([P, N, PACK], F32, name="t2", bufs=2)
+            nc.scalar.activation(out=t2s[m][:], in_=ts[m][:], func=ACT.Square)
+
+        def slope(m):
+            ds[m] = work.tile([P, N, PACK], F32, name="slope_t")
+            nc.scalar.activation(out=ds[m][:], in_=t2s[m][:], func=ACT.Identity, bias=minus_one[:])
+
+        def make_p(m):
+            ps[m] = work.tile([P, SUB, PACK, P], F32, name="p_t", bufs=2)
+            nc.gpsimd.tensor_tensor(
+                out=ps[m][:],
+                in0=ks[m][:].rearrange("r s (c t) -> r s t c", t=PACK),
+                in1=js[m][:].rearrange("r s (c t) -> r s t c", t=PACK),
+                op=ALU.mult,
+            )
+
+        def turn_p(m):
+            for s in range(SUB):
+                pb[m, s] = psum.tile([P, PACK, P], F32, name="bank_p%d" % s)
+                for t in range(PACK):
+                    nc.tensor.transpose(pb[m, s][:, t, :], ps[m][:, s, t, :], ident[:])
+
+        def make_g(m):
+            gs[m] = work.tile([P, N, PACK], BF16, name="g_t", bufs=2, align_bytes=64)
+            nc.vector.tensor_tensor(out=split(gs[m]), in0=split(ds[m]), in1=pairs(kb[m]), op=ALU.mult)
+
+        def quant(src, name):
+            codes = work.tile([P, N], U32, name="codes_" + name, bufs=2, align_bytes=64)
+            scales = work.tile([P, N], U8, name="scales_" + name, bufs=2, align_bytes=64)
+            nc.vector.quantize_mx(
+                out=codes[:].bitcast(FP8X4), scales=scales[:], in_=src[:].rearrange("p n t -> p (n t)")
+            )
+            return codes, scales
+
+        def make_q(m, s):
+            if s == 0:
+                qs[m] = work.tile([P, SUB, P, PACK], F32, name="q_t", bufs=2)
+            nc.vector.scalar_tensor_tensor(
+                out=qs[m][:, s],
+                in0=ts[m][:, s * P : (s + 1) * P, :],
+                scalar=2.0,
+                in1=pb[m, s][:].rearrange("p t r -> p r t"),
+                op0=ALU.mult,
+                op1=ALU.mult,
+            )
+
+        def mm_v(m):
+            codes, scales = gq[m]
+            for s in range(SUB):
+                cols = slice(s * P, (s + 1) * P)
+                vb[m, s] = psum.tile([P, PACK, P], F32, name="bank_v%d" % s)
+                for t in range(PACK):
+                    chans = slice(t * P, (t + 1) * P)
+                    nc.tensor.matmul_mx(
+                        out=vb[m, s][:, t, :],
+                        lhsT=wj_codes[:, chans].bitcast(FP8X4),
+                        lhsT_scale=wj_scales[:, chans],
+                        rhs=codes[:, cols].bitcast(FP8X4),
+                        rhs_scale=scales[:, cols],
+                        start=True,
+                        stop=True,
+                    )
+
+        def make_w(m, s):
+            if s == 0:
+                ws[m] = work.tile([P, SUB, P, PACK], F32, name="w_t", bufs=2)
+            nc.vector.tensor_tensor(
+                out=ws[m][:, s], in0=vb[m, s][:].rearrange("p t r -> p r t"), in1=qs[m][:, s], op=ALU.add
+            )
+
+        def make_u(m):
+            us[m] = work.tile([P, N, PACK], BF16, name="u_t", bufs=2, align_bytes=64)
+            nc.vector.tensor_tensor(
+                out=us[m][:].rearrange("p n t -> p (n t)"),
+                in0=ds[m][:].rearrange("p n t -> p (n t)"),
+                in1=ws[m][:].rearrange("p s r t -> p (s r t)"),
+                op=ALU.mult,
+            )
+
+        def mm_o(m):
+            codes, scales = uq[m]
+            for s in range(SUB):
+                cols = slice(s * P, (s + 1) * P)
+                ob[m, s] = psum.tile([P, D], F32, name="bank_o%d" % s)
+                nc.tensor.matmul_mx(
+                    out=ob[m, s][:],
+                    lhsT=codes[:, cols].bitcast(FP8X4),
+                    lhsT_scale=scales[:, cols],
+                    rhs=wi_codes[:].bitcast(FP8X4),
+                    rhs_scale=wi_scales[:],
+                    start=True,
+                    stop=True,
+                )
+
+        def copy_out(m, s, vector=False):
+            if s == 0:
+                outs[m] = work.tile([P, SUB, D], F32, name="o_t")
+            if vector:
+                nc.vector.tensor_copy(out=outs[m][:, s], in_=ob[m, s][:])
+            else:
+                nc.scalar.copy(out=outs[m][:, s], in_=ob[m, s][:])
+
+        def store(m):
+            nc.sync.dma_start(out=o_h[m], in_=outs[m][:])
+
+        load_x(0)
+        nc.sync.dma_start(out=wj_raw[:], in_=w_j.rearrange("(m t) k -> m t k", t=PACK))
+        nc.sync.dma_start(out=wi_byte[:], in_=w_i_bytes.rearrange("(c m) k -> m c k", m=P))
+        load_k(0)
+        load_j(0)
+        nc.sync.dma_start(out=wi_sc[:], in_=w_i_scale.rearrange("o (p t) -> p (o t)", t=PACK))
+        load(1)
+        load(2)
+        load(3)
+
+        make_identity(nc, ident[:])
+        nc.vector.memset(minus_one[:], -1.0)
+        nc.scalar.activation(out=warm[:], in_=minus_one[:], func=ACT.Tanh)
+
+        make_p(0)
+        make_p(1)
+
+        def turn_w(src, half, bank):
+            words = src[:].rearrange("m c k -> m (c k)").bitcast(F32).rearrange("m (c w) -> m c w", c=PACK)
+            for u in range(2):
+                for c in range(2):
+                    nc.tensor.transpose(bank[:, u, c, :], words[:, 2 * half + c, u : D // 2 : 2], ident[:])
+
+        turn_x(0)
+        tanh(0)
+        square(0)
+        slope(0)
+        wj_bank = [psum.tile([P, 2, 2, P], F32, name="bank_o%d" % h) for h in range(2)]
+        for h in range(2):
+            turn_w(wj_raw, h, wj_bank[h])
+        nc.vector.tensor_copy(out=wi_val[:], in_=wi_byte[:].bitcast(FP8))
+        for h in range(2):
+            nc.vector.tensor_copy(
+                out=wj_grp[:, 2 * h * P : 2 * (h + 1) * P, :].rearrange("p n t -> p (n t)").bitcast(F32).rearrange("p (n u) -> p n u", u=2),
+                in_=wj_bank[h][:].rearrange("p u c m -> p (c m) u"),
+            )
+        turn_k(0)
+        turn_x(1)
+        tanh(1)
+        square(1)
+        slope(1)
+        wi_bank = [psum.tile([P, 2, 2, P], F32, name="bank_v%d" % h) for h in range(2)]
+        for h in range(2):
+            turn_w(wi_val, h, wi_bank[h])
+        scale_all = wi_sc[:].rearrange("p (u e) -> p u e", u=2).unsqueeze(1).to_broadcast([P, N, 2, 2])
+
+        def scale_wi(h):
+            nc.vector.tensor_tensor(
+                out=wi_grp[:, h * N : (h + 1) * N, :].rearrange("p n (u e) -> p n u e", u=2),
+                in0=pairs(wi_bank[h]),
+                in1=scale_all,
+                op=ALU.mult,
+            )
+
+        def quant_w(codes, scales, src):
+            nc.vector.quantize_mx(
+                out=codes[:].bitcast(FP8X4), scales=scales[:], in_=src[:].rearrange("p n t -> p (n t)")
+            )
+
+        scale_wi(0)
+        quant_w(wj_codes, wj_scales, wj_grp)
+        make_g(0)
+        scale_wi(1)
+        gq[0] = quant(gs[0], "g")
+        turn_p(0)
+        turn_k(1)
+        turn_x(2)
+        mm_v(0)
+        make_q(0, 0)
+        make_q(0, 1)
+        quant_w(wi_codes, wi_scales, wi_grp)
+        make_p(2)
+
+        for m in range(MACROS):
+            nxt = m + 1 < MACROS
+            load(m + 4)
+            if nxt:
+                make_g(m + 1)
+            if m + 2 < MACROS:
+                tanh(m + 2)
+            if m >= 1:
+                mm_o(m - 1)
+                copy_out(m - 1, 0)
+            if nxt:
+                turn_p(m + 1)
+            if m + 3 < MACROS:
+                make_p(m + 3)
+            if m + 2 < MACROS:
+                turn_k(m + 2)
+            if m + 3 < MACROS:
+                turn_x(m + 3)
+            make_w(m, 0)
+            make_w(m, 1)
+            if m + 2 < MACROS:
+                square(m + 2)
+            if m >= 1:
+                copy_out(m - 1, 1)
+                store(m - 1)
+            if m + 2 < MACROS:
+                slope(m + 2)
+            if nxt:
+                make_q(m + 1, 0)
+                make_q(m + 1, 1)
+            make_u(m)
+            if nxt:
+                gq[m + 1] = quant(gs[m + 1], "g")
+            uq[m] = quant(us[m], "u")
+            if nxt:
+                mm_v(m + 1)
+
+        last = MACROS - 1
+        mm_o(last)
+        copy_out(last, 0)
+        copy_out(last, 1, vector=True)
+        store(last)

@@ -31,13 +31,13 @@ def tile_inimnetdisc_pa_t_kernel(tc, x, phi_j, phi_k, w_i_bytes, w_i_scale, w_j,
 
     with ExitStack() as ctx:
         keep = ctx.enter_context(tc.tile_pool(name="keep", bufs=1))
-        loads = ctx.enter_context(tc.tile_pool(name="loads", bufs=6))
-        work = ctx.enter_context(tc.tile_pool(name="work", bufs=3))
+        loads = ctx.enter_context(tc.tile_pool(name="loads", bufs=8))
+        work = ctx.enter_context(tc.tile_pool(name="work", bufs=2))
         psum = ctx.enter_context(tc.psum_pool(name="psum", bufs=1))
         ctx.enter_context(tc.manual_schedule())
 
         ident = keep.tile([P, P], F32, name="ident")
-        minus_one = keep.tile([P, 1], F32, name="minus_one")
+        zero = keep.tile([P, 1], F32, name="zero")
         warm = keep.tile([P, 1], F32, name="warm")
         wj_raw = keep.tile([P, PACK, D], BF16, name="wj_raw")
         wi_byte = keep.tile([P, PACK, D], U8, name="wi_byte")
@@ -50,10 +50,10 @@ def tile_inimnetdisc_pa_t_kernel(tc, x, phi_j, phi_k, w_i_bytes, w_i_scale, w_j,
         wi_codes = keep.tile([P, D], U32, name="wi_codes", align_bytes=64)
         wi_scales = keep.tile([P, D], U8, name="wi_scales", align_bytes=64)
 
-        xs, js, ks, ps = {}, {}, {}, {}
-        ts, ds, gs, qs, ws, us = {}, {}, {}, {}, {}, {}
-        t2s, gq, uq, outs = {}, {}, {}, {}
-        xb, kb, pb, vb, ob = {}, {}, {}, {}, {}
+        xs, js, ks = {}, {}, {}
+        ts, t2s, gs, tjs, at, bt = {}, {}, {}, {}, {}, {}
+        gg, ug, gq, uq, outs = {}, {}, {}, {}, {}
+        gb, ub, vb, ob = {}, {}, {}, {}
 
         def load_x(m):
             xs[m] = loads.tile([P, SUB, D], BF16, name="x_in")
@@ -73,152 +73,128 @@ def tile_inimnetdisc_pa_t_kernel(tc, x, phi_j, phi_k, w_i_bytes, w_i_scale, w_j,
                 load_k(m)
                 load_j(m)
 
-        def turn(src, bank):
-            words = src[:].rearrange("r s d -> r (s d)").bitcast(F32).rearrange("r (s w) -> r s w", s=SUB)
-            for u in range(2):
-                for s in range(SUB):
-                    nc.tensor.transpose(bank[:, u, s, :], words[:, s, u : D // 2 : 2], ident[:])
-
-        def turn_x(m):
-            xb[m] = psum.tile([P, 2, SUB, P], F32, name="bank_x")
-            turn(xs[m], xb[m])
-
-        def turn_k(m):
-            kb[m] = psum.tile([P, 2, SUB, P], F32, name="bank_k")
-            turn(ks[m], kb[m])
-
-        def pairs(bank):
-            return bank[:].rearrange("p u s r -> p (u s r)").bitcast(BF16).rearrange("p (u n e) -> p n u e", u=2, e=2)
-
-        def split(tile):
-            return tile[:].rearrange("p n (u e) -> p n u e", u=2)
-
         def tanh(m):
-            ts[m] = work.tile([P, N, PACK], F32, name="t")
-            nc.scalar.activation(out=split(ts[m]), in_=pairs(xb[m]), func=ACT.Tanh)
+            if m < MACROS:
+                ts[m] = work.tile([P, SUB, PACK, P], F32, name="t", bufs=3)
+                nc.scalar.activation(out=ts[m][:], in_=xs[m][:].rearrange("r s (c t) -> r s t c", t=PACK), func=ACT.Tanh)
 
         def square(m):
-            t2s[m] = work.tile([P, N, PACK], F32, name="t2", bufs=2)
-            nc.scalar.activation(out=t2s[m][:], in_=ts[m][:], func=ACT.Square)
-
-        def slope(m):
-            ds[m] = work.tile([P, N, PACK], F32, name="slope_t")
-            nc.scalar.activation(out=ds[m][:], in_=t2s[m][:], func=ACT.Identity, bias=minus_one[:])
-
-        def make_p(m):
-            ps[m] = work.tile([P, SUB, PACK, P], F32, name="p_t", bufs=2)
-            nc.gpsimd.tensor_tensor(
-                out=ps[m][:],
-                in0=ks[m][:].rearrange("r s (c t) -> r s t c", t=PACK),
-                in1=js[m][:].rearrange("r s (c t) -> r s t c", t=PACK),
-                op=ALU.mult,
-            )
-
-        def turn_p(m):
-            for s in range(SUB):
-                pb[m, s] = psum.tile([P, PACK, P], F32, name="bank_p%d" % s)
-                for t in range(PACK):
-                    nc.tensor.transpose(pb[m, s][:, t, :], ps[m][:, s, t, :], ident[:])
+            if m < MACROS:
+                t2s[m] = work.tile([P, SUB, PACK, P], F32, name="t2", bufs=3)
+                nc.scalar.activation(out=t2s[m][:], in_=ts[m][:], func=ACT.Square)
 
         def make_g(m):
-            gs[m] = work.tile([P, N, PACK], BF16, name="g_t", bufs=2, align_bytes=64)
-            nc.vector.tensor_tensor(out=split(gs[m]), in0=split(ds[m]), in1=pairs(kb[m]), op=ALU.mult)
+            gs[m] = work.tile([P, SUB, PACK, P], F32, name="g")
+            for s in range(SUB):
+                nc.vector.scalar_tensor_tensor(
+                    out=gs[m][:, s],
+                    in0=t2s[m][:, s],
+                    scalar=-1.0,
+                    in1=ks[m][:, s].rearrange("r (c t) -> r t c", t=PACK),
+                    op0=ALU.add,
+                    op1=ALU.mult,
+                )
+
+        def make_tj(m):
+            tjs[m] = work.tile([P, SUB, PACK, P], F32, name="tj")
+            nc.vector.tensor_tensor(
+                out=tjs[m][:], in0=ts[m][:], in1=js[m][:].rearrange("r s (c t) -> r s t c", t=PACK), op=ALU.mult
+            )
+
+        def make_b(m):
+            bt[m] = work.tile([P, SUB, PACK, P], F32, name="b_t")
+            flat = "r s t c -> r (s t c)"
+            nc.vector.scalar_tensor_tensor(
+                out=bt[m][:].rearrange(flat),
+                in0=tjs[m][:].rearrange(flat),
+                scalar=2.0,
+                in1=gs[m][:].rearrange(flat),
+                op0=ALU.mult,
+                op1=ALU.mult,
+            )
+
+        def make_a(m):
+            at[m] = work.tile([P, SUB, PACK, P], F32, name="a_t")
+            for s in range(SUB):
+                nc.vector.scalar_tensor_tensor(
+                    out=at[m][:, s],
+                    in0=t2s[m][:, s],
+                    scalar=-1.0,
+                    in1=vb[m, s][:],
+                    op0=ALU.add,
+                    op1=ALU.mult,
+                )
+
+        def turn_g(m):
+            for s in range(SUB):
+                gb[m, s] = psum.tile([P, PACK, P], F32, name="bank_g%d" % s)
+                for t in range(PACK):
+                    nc.tensor.transpose(gb[m, s][:, t, :], gs[m][:, s, t, :], ident[:])
+
+        def turn_u(m):
+            for s in range(SUB):
+                ub[m, s] = psum.tile([P, PACK, P], F32, name="bank_u%d" % s)
+                for t in range(PACK):
+                    nc.tensor.matmul(
+                        ub[m, s][:, t, :], lhsT=bt[m][:, s, t, :], rhs=ident[:], is_transpose=True, start=True, stop=False
+                    )
+                    nc.tensor.matmul(
+                        ub[m, s][:, t, :], lhsT=at[m][:, s, t, :], rhs=ident[:], is_transpose=True, start=False, stop=True
+                    )
+
+        def copy_g(m, s):
+            if s == 0:
+                gg[m] = work.tile([P, N, PACK], BF16, name="g_grp", align_bytes=64)
+            nc.scalar.copy(out=gg[m][:, s * P : (s + 1) * P, :], in_=gb[m, s][:].rearrange("p t r -> p r t"))
+
+        def copy_u(m, s, vector=False):
+            if s == 0:
+                ug[m] = work.tile([P, N, PACK], BF16, name="u_grp", align_bytes=64)
+            dst = ug[m][:, s * P : (s + 1) * P, :]
+            src = ub[m, s][:].rearrange("p t r -> p r t")
+            if vector:
+                nc.vector.tensor_copy(out=dst, in_=src)
+            else:
+                nc.scalar.copy(out=dst, in_=src)
 
         def quant(src, name):
-            codes = work.tile([P, N], U32, name="codes_" + name, bufs=2, align_bytes=64)
-            scales = work.tile([P, N], U8, name="scales_" + name, bufs=2, align_bytes=64)
+            codes = work.tile([P, N], U32, name="codes_" + name, align_bytes=64)
+            scales = work.tile([P, N], U8, name="scales_" + name, align_bytes=64)
             nc.vector.quantize_mx(
                 out=codes[:].bitcast(FP8X4), scales=scales[:], in_=src[:].rearrange("p n t -> p (n t)")
             )
             return codes, scales
 
-        def make_q(m, s):
-            if s == 0:
-                qs[m] = work.tile([P, SUB, P, PACK], F32, name="q_t", bufs=2)
-            nc.vector.scalar_tensor_tensor(
-                out=qs[m][:, s],
-                in0=ts[m][:, s * P : (s + 1) * P, :],
-                scalar=2.0,
-                in1=pb[m, s][:].rearrange("p t r -> p r t"),
-                op0=ALU.mult,
-                op1=ALU.mult,
+        def mm(operand, w_codes, w_scales, bank, s):
+            codes, scales = operand
+            cols = slice(s * P, (s + 1) * P)
+            nc.tensor.matmul_mx(
+                out=bank,
+                lhsT=codes[:, cols].bitcast(FP8X4),
+                lhsT_scale=scales[:, cols],
+                rhs=w_codes[:].bitcast(FP8X4),
+                rhs_scale=w_scales[:],
+                start=True,
+                stop=True,
             )
 
         def mm_v(m):
-            codes, scales = gq[m]
             for s in range(SUB):
-                cols = slice(s * P, (s + 1) * P)
                 vb[m, s] = psum.tile([P, PACK, P], F32, name="bank_v%d" % s)
-                for t in range(PACK):
-                    chans = slice(t * P, (t + 1) * P)
-                    nc.tensor.matmul_mx(
-                        out=vb[m, s][:, t, :],
-                        lhsT=wj_codes[:, chans].bitcast(FP8X4),
-                        lhsT_scale=wj_scales[:, chans],
-                        rhs=codes[:, cols].bitcast(FP8X4),
-                        rhs_scale=scales[:, cols],
-                        start=True,
-                        stop=True,
-                    )
-
-        def make_w(m, s):
-            if s == 0:
-                ws[m] = work.tile([P, SUB, P, PACK], F32, name="w_t", bufs=2)
-            nc.vector.tensor_tensor(
-                out=ws[m][:, s], in0=vb[m, s][:].rearrange("p t r -> p r t"), in1=qs[m][:, s], op=ALU.add
-            )
-
-        def make_u(m):
-            us[m] = work.tile([P, N, PACK], BF16, name="u_t", bufs=2, align_bytes=64)
-            nc.vector.tensor_tensor(
-                out=us[m][:].rearrange("p n t -> p (n t)"),
-                in0=ds[m][:].rearrange("p n t -> p (n t)"),
-                in1=ws[m][:].rearrange("p s r t -> p (s r t)"),
-                op=ALU.mult,
-            )
+                mm(gq[m], wj_codes, wj_scales, vb[m, s][:].rearrange("r t c -> r (t c)"), s)
 
         def mm_o(m):
-            codes, scales = uq[m]
             for s in range(SUB):
-                cols = slice(s * P, (s + 1) * P)
                 ob[m, s] = psum.tile([P, D], F32, name="bank_o%d" % s)
-                nc.tensor.matmul_mx(
-                    out=ob[m, s][:],
-                    lhsT=codes[:, cols].bitcast(FP8X4),
-                    lhsT_scale=scales[:, cols],
-                    rhs=wi_codes[:].bitcast(FP8X4),
-                    rhs_scale=wi_scales[:],
-                    start=True,
-                    stop=True,
-                )
+                mm(uq[m], wi_codes, wi_scales, ob[m, s][:], s)
 
         def copy_out(m, s, vector=False):
             if s == 0:
-                outs[m] = work.tile([P, SUB, D], F32, name="o_t")
+                outs[m] = work.tile([P, SUB, D], F32, name="o_t", bufs=3)
             if vector:
                 nc.vector.tensor_copy(out=outs[m][:, s], in_=ob[m, s][:])
             else:
                 nc.scalar.copy(out=outs[m][:, s], in_=ob[m, s][:])
-
-        def store(m):
-            nc.sync.dma_start(out=o_h[m], in_=outs[m][:])
-
-        load_x(0)
-        nc.sync.dma_start(out=wj_raw[:], in_=w_j.rearrange("(m t) k -> m t k", t=PACK))
-        nc.sync.dma_start(out=wi_byte[:], in_=w_i_bytes.rearrange("(c m) k -> m c k", m=P))
-        load_k(0)
-        load_j(0)
-        nc.sync.dma_start(out=wi_sc[:], in_=w_i_scale.rearrange("o (p t) -> p (o t)", t=PACK))
-        load(1)
-        load(2)
-        load(3)
-
-        make_identity(nc, ident[:])
-        nc.vector.memset(minus_one[:], -1.0)
-        nc.scalar.activation(out=warm[:], in_=minus_one[:], func=ACT.Tanh)
-
-        make_p(0)
-        make_p(1)
 
         def turn_w(src, half, bank):
             words = src[:].rearrange("m c k -> m (c k)").bitcast(F32).rearrange("m (c w) -> m c w", c=PACK)
@@ -226,95 +202,99 @@ def tile_inimnetdisc_pa_t_kernel(tc, x, phi_j, phi_k, w_i_bytes, w_i_scale, w_j,
                 for c in range(2):
                     nc.tensor.transpose(bank[:, u, c, :], words[:, 2 * half + c, u : D // 2 : 2], ident[:])
 
-        turn_x(0)
-        tanh(0)
-        square(0)
-        slope(0)
-        wj_bank = [psum.tile([P, 2, 2, P], F32, name="bank_o%d" % h) for h in range(2)]
-        for h in range(2):
-            turn_w(wj_raw, h, wj_bank[h])
-        nc.vector.tensor_copy(out=wi_val[:], in_=wi_byte[:].bitcast(FP8))
-        for h in range(2):
-            nc.vector.tensor_copy(
-                out=wj_grp[:, 2 * h * P : 2 * (h + 1) * P, :].rearrange("p n t -> p (n t)").bitcast(F32).rearrange("p (n u) -> p n u", u=2),
-                in_=wj_bank[h][:].rearrange("p u c m -> p (c m) u"),
-            )
-        turn_k(0)
-        turn_x(1)
-        tanh(1)
-        square(1)
-        slope(1)
-        wi_bank = [psum.tile([P, 2, 2, P], F32, name="bank_v%d" % h) for h in range(2)]
-        for h in range(2):
-            turn_w(wi_val, h, wi_bank[h])
-        scale_all = wi_sc[:].rearrange("p (u e) -> p u e", u=2).unsqueeze(1).to_broadcast([P, N, 2, 2])
-
-        def scale_wi(h):
-            nc.vector.tensor_tensor(
-                out=wi_grp[:, h * N : (h + 1) * N, :].rearrange("p n (u e) -> p n u e", u=2),
-                in0=pairs(wi_bank[h]),
-                in1=scale_all,
-                op=ALU.mult,
-            )
-
         def quant_w(codes, scales, src):
             nc.vector.quantize_mx(
                 out=codes[:].bitcast(FP8X4), scales=scales[:], in_=src[:].rearrange("p n t -> p (n t)")
             )
 
-        scale_wi(0)
-        quant_w(wj_codes, wj_scales, wj_grp)
+        load_x(0)
+        nc.sync.dma_start(out=wj_raw[:], in_=w_j.rearrange("(m t) k -> m t k", t=PACK))
+        load_k(0)
+        load_j(0)
+        load_x(1)
+        nc.sync.dma_start(out=wi_byte[:], in_=w_i_bytes.rearrange("(c m) k -> m c k", m=P))
+        nc.sync.dma_start(out=wi_sc[:], in_=w_i_scale.rearrange("o (p t) -> p (o t)", t=PACK))
+        load_k(1)
+        load_j(1)
+        load(2)
+        load(3)
+        load(4)
+
+        nc.vector.memset(zero[:], 0.0)
+        nc.scalar.activation(out=warm[:], in_=zero[:], func=ACT.Tanh)
+        make_identity(nc, ident[:])
+
+        tanh(0)
+        square(0)
+        wj_bank = [psum.tile([P, 2, 2, P], F32, name="bank_o%d" % h) for h in range(2)]
+        for h in range(2):
+            turn_w(wj_raw, h, wj_bank[h])
+        for h in range(2):
+            dst = wj_grp[:, h * N : (h + 1) * N, :].rearrange("p n t -> p (n t)").bitcast(F32).rearrange("p (n u) -> p n u", u=2)
+            src = wj_bank[h][:].rearrange("p u c m -> p (c m) u")
+            nc.vector.tensor_copy(out=dst, in_=src)
         make_g(0)
-        scale_wi(1)
-        gq[0] = quant(gs[0], "g")
-        turn_p(0)
-        turn_k(1)
-        turn_x(2)
-        mm_v(0)
-        make_q(0, 0)
-        make_q(0, 1)
-        quant_w(wi_codes, wi_scales, wi_grp)
-        make_p(2)
+        turn_g(0)
+        tanh(1)
+        copy_g(0, 0)
+        copy_g(0, 1)
+        square(1)
+        quant_w(wj_codes, wj_scales, wj_grp)
+        make_tj(0)
+        gq[0] = quant(gg[0], "g")
+        make_b(0)
+        nc.vector.tensor_copy(out=wi_val[:], in_=wi_byte[:].bitcast(FP8))
+        tanh(2)
 
         for m in range(MACROS):
             nxt = m + 1 < MACROS
-            load(m + 4)
+            last = not nxt
+            load(m + 5)
+            square(m + 2)
+            mm_v(m)
+            if nxt:
+                make_tj(m + 1)
+            if m >= 1:
+                uq[m - 1] = quant(ug[m - 1], "u")
+                mm_o(m - 1)
             if nxt:
                 make_g(m + 1)
-            if m + 2 < MACROS:
-                tanh(m + 2)
+                turn_g(m + 1)
+            tanh(m + 3)
+            if nxt:
+                copy_g(m + 1, 0)
+                copy_g(m + 1, 1)
+            make_a(m)
+            turn_u(m)
             if m >= 1:
-                mm_o(m - 1)
                 copy_out(m - 1, 0)
-            if nxt:
-                turn_p(m + 1)
-            if m + 3 < MACROS:
-                make_p(m + 3)
-            if m + 2 < MACROS:
-                turn_k(m + 2)
-            if m + 3 < MACROS:
-                turn_x(m + 3)
-            make_w(m, 0)
-            make_w(m, 1)
-            if m + 2 < MACROS:
-                square(m + 2)
-            if m >= 1:
                 copy_out(m - 1, 1)
-                store(m - 1)
-            if m + 2 < MACROS:
-                slope(m + 2)
+                nc.sync.dma_start(out=o_h[m - 1], in_=outs[m - 1][:])
+            copy_u(m, 0)
+            copy_u(m, 1, vector=last)
             if nxt:
-                make_q(m + 1, 0)
-                make_q(m + 1, 1)
-            make_u(m)
+                make_b(m + 1)
+            if m == 0:
+                wi_bank = [psum.tile([P, 2, 2, P], F32, name="bank_o%d" % h) for h in range(2)]
+                scale_all = wi_sc[:].rearrange("p (u e) -> p u e", u=2).unsqueeze(1).to_broadcast([P, N, 2, 2])
+                for h in range(2):
+                    turn_w(wi_val, h, wi_bank[h])
+                for h in range(2):
+                    nc.vector.tensor_tensor(
+                        out=wi_grp[:, h * N : (h + 1) * N, :].rearrange("p n (u e) -> p n u e", u=2),
+                        in0=wi_bank[h][:].rearrange("p u c m -> p (u c m)").bitcast(BF16).rearrange("p (u n e) -> p n u e", u=2, e=2),
+                        in1=scale_all,
+                        op=ALU.mult,
+                    )
             if nxt:
-                gq[m + 1] = quant(gs[m + 1], "g")
-            uq[m] = quant(us[m], "u")
-            if nxt:
-                mm_v(m + 1)
+                gq[m + 1] = quant(gg[m + 1], "g")
+            if m == 0:
+                quant_w(wi_codes, wi_scales, wi_grp)
 
-        last = MACROS - 1
-        mm_o(last)
-        copy_out(last, 0)
-        copy_out(last, 1, vector=True)
-        store(last)
+        end = MACROS - 1
+        uq[end] = quant(ug[end], "u")
+        mm_o(end)
+        copy_out(end, 0)
+        copy_out(end, 1, vector=True)
+        for s in range(SUB):
+            nc.sync.dma_start(out=o_h[end][:, s], in_=outs[end][:, s])

@@ -73,19 +73,29 @@ def tile_inimnetdisc_pa_t_kernel(tc, x, phi_j, phi_k, w_i_bytes, w_i_scale, w_j,
                 load_k(m)
                 load_j(m)
 
-        def tanh(m):
-            if m < MACROS:
-                ts[m] = work.tile([P, SUB, PACK, P], F32, name="t", bufs=3)
-                nc.scalar.activation(out=ts[m][:], in_=xs[m][:].rearrange("r s (c t) -> r s t c", t=PACK), func=ACT.Tanh)
+        def rows(s):
+            return slice(0, SUB) if s is None else slice(s, s + 1)
 
-        def square(m):
+        def tanh(m, s=None):
             if m < MACROS:
-                t2s[m] = work.tile([P, SUB, PACK, P], F32, name="t2", bufs=3)
-                nc.scalar.activation(out=t2s[m][:], in_=ts[m][:], func=ACT.Square)
+                if not s:
+                    ts[m] = work.tile([P, SUB, PACK, P], F32, name="t", bufs=3)
+                nc.scalar.activation(
+                    out=ts[m][:, rows(s)],
+                    in_=xs[m][:, rows(s)].rearrange("r s (c t) -> r s t c", t=PACK),
+                    func=ACT.Tanh,
+                )
 
-        def make_g(m):
-            gs[m] = work.tile([P, SUB, PACK, P], F32, name="g")
-            for s in range(SUB):
+        def square(m, s=None):
+            if m < MACROS:
+                if not s:
+                    t2s[m] = work.tile([P, SUB, PACK, P], F32, name="t2", bufs=3)
+                nc.scalar.activation(out=t2s[m][:, rows(s)], in_=ts[m][:, rows(s)], func=ACT.Square)
+
+        def make_g(m, s):
+            if m < MACROS:
+                if s == 0:
+                    gs[m] = work.tile([P, SUB, PACK, P], F32, name="g")
                 nc.vector.scalar_tensor_tensor(
                     out=gs[m][:, s],
                     in0=t2s[m][:, s],
@@ -96,56 +106,58 @@ def tile_inimnetdisc_pa_t_kernel(tc, x, phi_j, phi_k, w_i_bytes, w_i_scale, w_j,
                 )
 
         def make_tj(m):
-            tjs[m] = work.tile([P, SUB, PACK, P], F32, name="tj")
-            nc.vector.tensor_tensor(
-                out=tjs[m][:], in0=ts[m][:], in1=js[m][:].rearrange("r s (c t) -> r s t c", t=PACK), op=ALU.mult
-            )
+            if m < MACROS:
+                tjs[m] = work.tile([P, SUB, PACK, P], F32, name="tj")
+                for s in range(SUB):
+                    nc.vector.scalar_tensor_tensor(
+                        out=tjs[m][:, s],
+                        in0=ts[m][:, s],
+                        scalar=2.0,
+                        in1=js[m][:, s].rearrange("r (c t) -> r t c", t=PACK),
+                        op0=ALU.mult,
+                        op1=ALU.mult,
+                    )
 
-        def make_b(m):
-            bt[m] = work.tile([P, SUB, PACK, P], F32, name="b_t")
-            flat = "r s t c -> r (s t c)"
+        def make_b(m, s, pool=False):
+            if m < MACROS:
+                if m not in bt:
+                    bt[m] = work.tile([P, SUB, PACK, P], F32, name="b_t")
+                if pool:
+                    nc.gpsimd.tensor_tensor(out=bt[m][:, s], in0=tjs[m][:, s], in1=gs[m][:, s], op=ALU.mult)
+                else:
+                    nc.vector.tensor_tensor(out=bt[m][:, s], in0=tjs[m][:, s], in1=gs[m][:, s], op=ALU.mult)
+
+        def make_a(m, s):
+            if s == 0:
+                at[m] = work.tile([P, SUB, PACK, P], F32, name="a_t")
             nc.vector.scalar_tensor_tensor(
-                out=bt[m][:].rearrange(flat),
-                in0=tjs[m][:].rearrange(flat),
-                scalar=2.0,
-                in1=gs[m][:].rearrange(flat),
-                op0=ALU.mult,
-                op1=ALU.mult,
+                out=at[m][:, s], in0=t2s[m][:, s], scalar=-1.0, in1=vb[m, s][:], op0=ALU.add, op1=ALU.mult
             )
 
-        def make_a(m):
-            at[m] = work.tile([P, SUB, PACK, P], F32, name="a_t")
-            for s in range(SUB):
-                nc.vector.scalar_tensor_tensor(
-                    out=at[m][:, s],
-                    in0=t2s[m][:, s],
-                    scalar=-1.0,
-                    in1=vb[m, s][:],
-                    op0=ALU.add,
-                    op1=ALU.mult,
-                )
-
-        def turn_g(m):
-            for s in range(SUB):
+        def turn_g(m, s):
+            if m < MACROS:
                 gb[m, s] = psum.tile([P, PACK, P], F32, name="bank_g%d" % s)
                 for t in range(PACK):
                     nc.tensor.transpose(gb[m, s][:, t, :], gs[m][:, s, t, :], ident[:])
 
-        def turn_u(m):
-            for s in range(SUB):
-                ub[m, s] = psum.tile([P, PACK, P], F32, name="bank_u%d" % s)
-                for t in range(PACK):
+        def turn_u(m, s):
+            ub[m, s] = psum.tile([P, PACK, P], F32, name="bank_u%d" % s)
+            for t in range(PACK):
+                for part, first in ((bt, True), (at, False)):
                     nc.tensor.matmul(
-                        ub[m, s][:, t, :], lhsT=bt[m][:, s, t, :], rhs=ident[:], is_transpose=True, start=True, stop=False
-                    )
-                    nc.tensor.matmul(
-                        ub[m, s][:, t, :], lhsT=at[m][:, s, t, :], rhs=ident[:], is_transpose=True, start=False, stop=True
+                        ub[m, s][:, t, :],
+                        lhsT=part[m][:, s, t, :],
+                        rhs=ident[:],
+                        is_transpose=True,
+                        start=first,
+                        stop=not first,
                     )
 
         def copy_g(m, s):
-            if s == 0:
-                gg[m] = work.tile([P, N, PACK], BF16, name="g_grp", align_bytes=64)
-            nc.scalar.copy(out=gg[m][:, s * P : (s + 1) * P, :], in_=gb[m, s][:].rearrange("p t r -> p r t"))
+            if m < MACROS:
+                if s == 0:
+                    gg[m] = work.tile([P, N, PACK], BF16, name="g_grp", align_bytes=64)
+                nc.scalar.copy(out=gg[m][:, s * P : (s + 1) * P, :], in_=gb[m, s][:].rearrange("p t r -> p r t"))
 
         def copy_u(m, s, vector=False):
             if s == 0:
@@ -157,13 +169,27 @@ def tile_inimnetdisc_pa_t_kernel(tc, x, phi_j, phi_k, w_i_bytes, w_i_scale, w_j,
             else:
                 nc.scalar.copy(out=dst, in_=src)
 
-        def quant(src, name):
-            codes = work.tile([P, N], U32, name="codes_" + name, align_bytes=64)
-            scales = work.tile([P, N], U8, name="scales_" + name, align_bytes=64)
+        def quant(done, src, m, s, name):
+            if not s:
+                done[m] = (
+                    work.tile([P, N], U32, name="codes_" + name, align_bytes=64),
+                    work.tile([P, N], U8, name="scales_" + name, align_bytes=64),
+                )
+            codes, scales = done[m]
+            cols = slice(0, N) if s is None else slice(s * P, (s + 1) * P)
             nc.vector.quantize_mx(
-                out=codes[:].bitcast(FP8X4), scales=scales[:], in_=src[:].rearrange("p n t -> p (n t)")
+                out=codes[:, cols].bitcast(FP8X4),
+                scales=scales[:, cols],
+                in_=src[m][:, cols, :].rearrange("p n t -> p (n t)"),
             )
-            return codes, scales
+
+        def quant_g(m, s=None):
+            if m < MACROS:
+                quant(gq, gg, m, s, "g")
+
+        def quant_u(m, s=None):
+            if m >= 0:
+                quant(uq, ug, m, s, "u")
 
         def mm(operand, w_codes, w_scales, bank, s):
             codes, scales = operand
@@ -178,23 +204,28 @@ def tile_inimnetdisc_pa_t_kernel(tc, x, phi_j, phi_k, w_i_bytes, w_i_scale, w_j,
                 stop=True,
             )
 
-        def mm_v(m):
-            for s in range(SUB):
+        def mm_v(m, s):
+            if m < MACROS:
                 vb[m, s] = psum.tile([P, PACK, P], F32, name="bank_v%d" % s)
                 mm(gq[m], wj_codes, wj_scales, vb[m, s][:].rearrange("r t c -> r (t c)"), s)
 
-        def mm_o(m):
-            for s in range(SUB):
+        def mm_o(m, s):
+            if m >= 0:
                 ob[m, s] = psum.tile([P, D], F32, name="bank_o%d" % s)
                 mm(uq[m], wi_codes, wi_scales, ob[m, s][:], s)
 
         def copy_out(m, s, vector=False):
-            if s == 0:
-                outs[m] = work.tile([P, SUB, D], F32, name="o_t", bufs=3)
-            if vector:
-                nc.vector.tensor_copy(out=outs[m][:, s], in_=ob[m, s][:])
-            else:
-                nc.scalar.copy(out=outs[m][:, s], in_=ob[m, s][:])
+            if m >= 0:
+                if s == 0:
+                    outs[m] = work.tile([P, SUB, D], F32, name="o_t", bufs=3)
+                if vector:
+                    nc.vector.tensor_copy(out=outs[m][:, s], in_=ob[m, s][:])
+                else:
+                    nc.scalar.copy(out=outs[m][:, s], in_=ob[m, s][:])
+
+        def store(m, s=None):
+            if m >= 0:
+                nc.sync.dma_start(out=o_h[m][:, rows(s)], in_=outs[m][:, rows(s)])
 
         def turn_w(src, half, bank):
             words = src[:].rearrange("m c k -> m (c k)").bitcast(F32).rearrange("m (c w) -> m c w", c=PACK)
@@ -202,99 +233,119 @@ def tile_inimnetdisc_pa_t_kernel(tc, x, phi_j, phi_k, w_i_bytes, w_i_scale, w_j,
                 for c in range(2):
                     nc.tensor.transpose(bank[:, u, c, :], words[:, 2 * half + c, u : D // 2 : 2], ident[:])
 
+        wbank = {}
+
+        def turn_wj(h):
+            wbank["j", h] = psum.tile([P, 2, 2, P], F32, name="bank_o%d" % h)
+            turn_w(wj_raw, h, wbank["j", h])
+
+        def copy_wj(h, vector=True):
+            dst = wj_grp[:, h * N : (h + 1) * N, :].rearrange("p n t -> p (n t)").bitcast(F32).rearrange("p (n u) -> p n u", u=2)
+            src = wbank["j", h][:].rearrange("p u c m -> p (c m) u")
+            if vector:
+                nc.vector.tensor_copy(out=dst, in_=src)
+            else:
+                nc.scalar.copy(out=dst, in_=src)
+
+        def widen(h):
+            nc.vector.tensor_copy(out=wi_val[:, 2 * h : 2 * h + 2], in_=wi_byte[:, 2 * h : 2 * h + 2].bitcast(FP8))
+
+        def turn_wi(h):
+            wbank["i", h] = psum.tile([P, 2, 2, P], F32, name="bank_o%d" % h)
+            turn_w(wi_val, h, wbank["i", h])
+
+        def scale_wi(h):
+            nc.vector.tensor_tensor(
+                out=wi_grp[:, h * N : (h + 1) * N, :].rearrange("p n (u e) -> p n u e", u=2),
+                in0=wbank["i", h][:].rearrange("p u c m -> p (u c m)").bitcast(BF16).rearrange("p (u n e) -> p n u e", u=2, e=2),
+                in1=wi_sc[:].rearrange("p (u e) -> p u e", u=2).unsqueeze(1).to_broadcast([P, N, 2, 2]),
+                op=ALU.mult,
+            )
+
+        def quant_wj():
+            quant_w(wj_codes, wj_scales, wj_grp)
+
+        def quant_wi():
+            quant_w(wi_codes, wi_scales, wi_grp)
+
+        def load_wj():
+            nc.sync.dma_start(out=wj_raw[:], in_=w_j.rearrange("(m t) k -> m t k", t=PACK))
+
+        def load_wi():
+            nc.sync.dma_start(out=wi_byte[:], in_=w_i_bytes.rearrange("(c m) k -> m c k", m=P))
+
+        def load_sc():
+            nc.sync.dma_start(out=wi_sc[:], in_=w_i_scale.rearrange("o (p t) -> p (o t)", t=PACK))
+
+        def prepare():
+            nc.vector.memset(zero[:], 0.0)
+            nc.scalar.activation(out=warm[:], in_=zero[:], func=ACT.Tanh)
+            make_identity(nc, ident[:])
+
         def quant_w(codes, scales, src):
             nc.vector.quantize_mx(
                 out=codes[:].bitcast(FP8X4), scales=scales[:], in_=src[:].rearrange("p n t -> p (n t)")
             )
-
-        load_x(0)
-        nc.sync.dma_start(out=wj_raw[:], in_=w_j.rearrange("(m t) k -> m t k", t=PACK))
-        load_k(0)
-        load_j(0)
-        load_x(1)
-        nc.sync.dma_start(out=wi_byte[:], in_=w_i_bytes.rearrange("(c m) k -> m c k", m=P))
-        nc.sync.dma_start(out=wi_sc[:], in_=w_i_scale.rearrange("o (p t) -> p (o t)", t=PACK))
-        load_k(1)
-        load_j(1)
-        load(2)
-        load(3)
-        load(4)
-
-        nc.vector.memset(zero[:], 0.0)
-        nc.scalar.activation(out=warm[:], in_=zero[:], func=ACT.Tanh)
-        make_identity(nc, ident[:])
-
-        tanh(0)
-        square(0)
-        wj_bank = [psum.tile([P, 2, 2, P], F32, name="bank_o%d" % h) for h in range(2)]
+        load_x(0); load_wi(); load_k(0); load_wj(); load_j(0); load_sc(); load_x(1); load_k(1); load_j(1)
+        for m in range(2, 5):
+            load(m)
+        prepare()
+        widen(0)
+        for s in range(SUB):
+            tanh(0, s)
+            square(0, s)
+            make_g(0, s)
         for h in range(2):
-            turn_w(wj_raw, h, wj_bank[h])
-        for h in range(2):
-            dst = wj_grp[:, h * N : (h + 1) * N, :].rearrange("p n t -> p (n t)").bitcast(F32).rearrange("p (n u) -> p n u", u=2)
-            src = wj_bank[h][:].rearrange("p u c m -> p (c m) u")
-            nc.vector.tensor_copy(out=dst, in_=src)
-        make_g(0)
-        turn_g(0)
-        tanh(1)
-        copy_g(0, 0)
-        copy_g(0, 1)
-        square(1)
-        quant_w(wj_codes, wj_scales, wj_grp)
+            turn_wj(h)
+        widen(1)
+        copy_wj(0); copy_wj(1, vector=False)
+        for s in range(SUB):
+            turn_g(0, s)
+            copy_g(0, s)
+        quant_wj()
         make_tj(0)
-        gq[0] = quant(gg[0], "g")
-        make_b(0)
-        nc.vector.tensor_copy(out=wi_val[:], in_=wi_byte[:].bitcast(FP8))
+        quant_g(0)
+        for s in range(SUB):
+            mm_v(0, s)
+        tanh(1)
+        square(1)
+        make_b(0, 0)
+        make_b(0, 1)
+        for h in range(2):
+            turn_wi(h)
         tanh(2)
-
         for m in range(MACROS):
-            nxt = m + 1 < MACROS
-            last = not nxt
+            last = m == MACROS - 1
             load(m + 5)
             square(m + 2)
-            mm_v(m)
-            if nxt:
-                make_tj(m + 1)
-            if m >= 1:
-                uq[m - 1] = quant(ug[m - 1], "u")
-                mm_o(m - 1)
-            if nxt:
-                make_g(m + 1)
-                turn_g(m + 1)
+            make_tj(m + 1)
+            quant_u(m - 1)
+            for s in range(SUB):
+                mm_o(m - 1, s)
+            for s in range(SUB):
+                make_g(m + 1, s)
+                turn_g(m + 1, s)
+            make_b(m + 1, 1, pool=True)
             tanh(m + 3)
-            if nxt:
-                copy_g(m + 1, 0)
-                copy_g(m + 1, 1)
-            make_a(m)
-            turn_u(m)
-            if m >= 1:
-                copy_out(m - 1, 0)
-                copy_out(m - 1, 1)
-                nc.sync.dma_start(out=o_h[m - 1], in_=outs[m - 1][:])
+            copy_g(m + 1, 0)
+            copy_g(m + 1, 1)
+            for s in range(SUB):
+                make_a(m, s)
+                turn_u(m, s)
+            copy_out(m - 1, 0)
+            copy_out(m - 1, 1, vector=True)
+            store(m - 1)
             copy_u(m, 0)
             copy_u(m, 1, vector=last)
-            if nxt:
-                make_b(m + 1)
+            make_b(m + 1, 0)
             if m == 0:
-                wi_bank = [psum.tile([P, 2, 2, P], F32, name="bank_o%d" % h) for h in range(2)]
-                scale_all = wi_sc[:].rearrange("p (u e) -> p u e", u=2).unsqueeze(1).to_broadcast([P, N, 2, 2])
-                for h in range(2):
-                    turn_w(wi_val, h, wi_bank[h])
-                for h in range(2):
-                    nc.vector.tensor_tensor(
-                        out=wi_grp[:, h * N : (h + 1) * N, :].rearrange("p n (u e) -> p n u e", u=2),
-                        in0=wi_bank[h][:].rearrange("p u c m -> p (u c m)").bitcast(BF16).rearrange("p (u n e) -> p n u e", u=2, e=2),
-                        in1=scale_all,
-                        op=ALU.mult,
-                    )
-            if nxt:
-                gq[m + 1] = quant(gg[m + 1], "g")
-            if m == 0:
-                quant_w(wi_codes, wi_scales, wi_grp)
-
-        end = MACROS - 1
-        uq[end] = quant(ug[end], "u")
-        mm_o(end)
-        copy_out(end, 0)
-        copy_out(end, 1, vector=True)
+                scale_wi(0); scale_wi(1)
+                quant_wi()
+            quant_g(m + 1)
+            for s in range(SUB):
+                mm_v(m + 1, s)
         for s in range(SUB):
-            nc.sync.dma_start(out=o_h[end][:, s], in_=outs[end][:, s])
+            quant_u(MACROS - 1, s)
+            mm_o(MACROS - 1, s)
+            copy_out(MACROS - 1, s, vector=(s == 1))
+            store(MACROS - 1, s)

@@ -59,6 +59,11 @@ def tile_inimnetdisc_pa_t_kernel(tc, x, phi_j, phi_k, w_i_bytes, w_i_scale, w_j,
             xs[m] = loads.tile([P, SUB, D], BF16, name="x_in")
             nc.sync.dma_start(out=xs[m][:], in_=x_h[m])
 
+        def load_x_half(s):
+            if s == 0:
+                xs[0] = loads.tile([P, SUB, D], BF16, name="x_in")
+            nc.sync.dma_start(out=xs[0][:, s], in_=x_h[0][:, s])
+
         def load_k(m):
             ks[m] = loads.tile([P, SUB, D], BF16, name="k_in")
             nc.sync.dma_start(out=ks[m][:], in_=k_h[m])
@@ -126,6 +131,23 @@ def tile_inimnetdisc_pa_t_kernel(tc, x, phi_j, phi_k, w_i_bytes, w_i_scale, w_j,
                     nc.gpsimd.tensor_tensor(out=bt[m][:, s], in0=tjs[m][:, s], in1=gs[m][:, s], op=ALU.mult)
                 else:
                     nc.vector.tensor_tensor(out=bt[m][:, s], in0=tjs[m][:, s], in1=gs[m][:, s], op=ALU.mult)
+
+        def make_bs(m, q, pool=False):
+            if m < MACROS:
+                if pool:
+                    bt[m] = work.tile([P, SUB, PACK, P], F32, name="b_t")
+                cols = slice(q, N * PACK) if pool else slice(0, q)
+                flat = "r s t c -> r (s t c)"
+                args = dict(
+                    out=bt[m][:].rearrange(flat)[:, cols],
+                    in0=tjs[m][:].rearrange(flat)[:, cols],
+                    in1=gs[m][:].rearrange(flat)[:, cols],
+                    op=ALU.mult,
+                )
+                if pool:
+                    nc.gpsimd.tensor_tensor(**args)
+                else:
+                    nc.vector.tensor_tensor(**args)
 
         def make_a(m, s):
             if s == 0:
@@ -247,8 +269,12 @@ def tile_inimnetdisc_pa_t_kernel(tc, x, phi_j, phi_k, w_i_bytes, w_i_scale, w_j,
             else:
                 nc.scalar.copy(out=dst, in_=src)
 
-        def widen(h):
-            nc.vector.tensor_copy(out=wi_val[:, 2 * h : 2 * h + 2], in_=wi_byte[:, 2 * h : 2 * h + 2].bitcast(FP8))
+        def widen(h, vector=True):
+            dst, src = wi_val[:, 2 * h : 2 * h + 2], wi_byte[:, 2 * h : 2 * h + 2].bitcast(FP8)
+            if vector:
+                nc.vector.tensor_copy(out=dst, in_=src)
+            else:
+                nc.scalar.copy(out=dst, in_=src)
 
         def turn_wi(h):
             wbank["i", h] = psum.tile([P, 2, 2, P], F32, name="bank_o%d" % h)
@@ -286,61 +312,68 @@ def tile_inimnetdisc_pa_t_kernel(tc, x, phi_j, phi_k, w_i_bytes, w_i_scale, w_j,
             nc.vector.quantize_mx(
                 out=codes[:].bitcast(FP8X4), scales=scales[:], in_=src[:].rearrange("p n t -> p (n t)")
             )
-        load_x(0); load_wi(); load_k(0); load_wj(); load_j(0); load_sc(); load_x(1); load_k(1); load_j(1)
+        BQ = 320
+        load_x_half(0); load_x_half(1); load_wi(); load_k(0); load_wj(); load_j(0); load_sc(); load_x(1); load_k(1); load_j(1)
         for m in range(2, 5):
             load(m)
         prepare()
-        widen(0)
         for s in range(SUB):
             tanh(0, s)
+        for s in range(SUB):
             square(0, s)
+        for s in range(SUB):
             make_g(0, s)
         for h in range(2):
             turn_wj(h)
-        widen(1)
-        copy_wj(0); copy_wj(1, vector=False)
+        widen(0, vector=False)
+        copy_wj(0, vector=False)
+        widen(1, vector=False)
+        make_tj(0)
+        for s in range(SUB):
+            make_b(0, s, pool=True)
+        copy_wj(1)
         for s in range(SUB):
             turn_g(0, s)
-            copy_g(0, s)
         quant_wj()
-        make_tj(0)
+        for h in range(2):
+            turn_wi(h)
+        tanh(1)
+        for s in range(SUB):
+            copy_g(0, s)
+        for h in range(2):
+            scale_wi(h)
         quant_g(0)
         for s in range(SUB):
             mm_v(0, s)
-        tanh(1)
-        square(1)
-        make_b(0, 0)
-        make_b(0, 1)
-        for h in range(2):
-            turn_wi(h)
+        quant_wi()
         tanh(2)
+        square(1)
         for m in range(MACROS):
-            last = m == MACROS - 1
             load(m + 5)
+            tanh(m + 3)
             square(m + 2)
             make_tj(m + 1)
             quant_u(m - 1)
             for s in range(SUB):
+                make_g(m + 1, s)
+            for s in range(SUB):
                 mm_o(m - 1, s)
             for s in range(SUB):
-                make_g(m + 1, s)
                 turn_g(m + 1, s)
-            make_b(m + 1, 1, pool=True)
-            tanh(m + 3)
-            copy_g(m + 1, 0)
-            copy_g(m + 1, 1)
+            make_bs(m + 1, BQ, pool=True)
+            if m >= MACROS - 2:
+                copy_out(m - 1, 0)
             for s in range(SUB):
                 make_a(m, s)
-                turn_u(m, s)
-            copy_out(m - 1, 0)
+                copy_g(m + 1, s)
+            if m < MACROS - 2:
+                copy_out(m - 1, 0)
             copy_out(m - 1, 1, vector=True)
             store(m - 1)
-            copy_u(m, 0)
-            copy_u(m, 1, vector=last)
-            make_b(m + 1, 0)
-            if m == 0:
-                scale_wi(0); scale_wi(1)
-                quant_wi()
+            make_bs(m + 1, BQ)
+            for s in range(SUB):
+                turn_u(m, s)
+                copy_u(m, s)
             quant_g(m + 1)
             for s in range(SUB):
                 mm_v(m + 1, s)

from contextlib import ExitStack

import concourse.mybir as mybir
from concourse.masks import make_identity

TOKENS, D = 4096, 512
P = 128
PACK = 4
SUB = 2
N = P * SUB
MACROS = TOKENS // N

FLOPS = 2 * 2 * TOKENS * D * D

F32 = mybir.dt.float32
BF16 = mybir.dt.bfloat16
U32 = mybir.dt.uint32
U8 = mybir.dt.uint8
FP8 = mybir.dt.float8_e4m3fn
FP8X4 = mybir.dt.float8_e4m3fn_x4
ACT = mybir.ActivationFunctionType
ALU = mybir.AluOpType


def tile_inimnetdisc_pa_t_kernel(tc, x, phi_j, phi_k, w_i_bytes, w_i_scale, w_j, out):
    nc = tc.nc
    x_h = x.rearrange("(m r s) d -> m r s d", r=P, s=SUB)
    j_h = phi_j.rearrange("(m r s) d -> m r s d", r=P, s=SUB)
    k_h = phi_k.rearrange("(m r s) d -> m r s d", r=P, s=SUB)
    o_h = out.rearrange("(m r s) d -> m r s d", r=P, s=SUB)

    with ExitStack() as ctx:
        keep = ctx.enter_context(tc.tile_pool(name="keep", bufs=1))
        loads = ctx.enter_context(tc.tile_pool(name="loads", bufs=8))
        work = ctx.enter_context(tc.tile_pool(name="work", bufs=2))
        psum = ctx.enter_context(tc.psum_pool(name="psum", bufs=1))
        ctx.enter_context(tc.manual_schedule())

        ident = keep.tile([P, P], F32, name="ident")
        zero = keep.tile([P, 1], F32, name="zero")
        warm = keep.tile([P, 1], F32, name="warm")
        wj_raw = keep.tile([P, PACK, D], BF16, name="wj_raw")
        wi_byte = keep.tile([P, PACK, D], U8, name="wi_byte")
        wi_val = keep.tile([P, PACK, D], BF16, name="wi_val")
        wi_sc = keep.tile([P, PACK], F32, name="wi_sc")
        wj_grp = keep.tile([P, D, PACK], BF16, name="wj_grp", align_bytes=64)
        wi_grp = keep.tile([P, D, PACK], BF16, name="wi_grp", align_bytes=64)
        wj_codes = keep.tile([P, D], U32, name="wj_codes", align_bytes=64)
        wj_scales = keep.tile([P, D], U8, name="wj_scales", align_bytes=64)
        wi_codes = keep.tile([P, D], U32, name="wi_codes", align_bytes=64)
        wi_scales = keep.tile([P, D], U8, name="wi_scales", align_bytes=64)

        xs, js, ks = {}, {}, {}
        ts, t2s, gs, tjs, at, bt = {}, {}, {}, {}, {}, {}
        gg, ug, gq, uq, outs = {}, {}, {}, {}, {}
        gb, ub, vb, ob = {}, {}, {}, {}

        def load_x(m):
            xs[m] = loads.tile([P, SUB, D], BF16, name="x_in")
            nc.sync.dma_start(out=xs[m][:], in_=x_h[m])

        def load_x_half(s):
            if s == 0:
                xs[0] = loads.tile([P, SUB, D], BF16, name="x_in")
            nc.sync.dma_start(out=xs[0][:, s], in_=x_h[0][:, s])

        def load_k(m):
            ks[m] = loads.tile([P, SUB, D], BF16, name="k_in")
            nc.sync.dma_start(out=ks[m][:], in_=k_h[m])

        def load_j(m):
            js[m] = loads.tile([P, SUB, D], BF16, name="j_in")
            nc.sync.dma_start(out=js[m][:], in_=j_h[m])

        def load(m):
            if m < MACROS:
                load_x(m)
                load_k(m)
                load_j(m)

        def rows(s):
            return slice(0, SUB) if s is None else slice(s, s + 1)

        def tanh(m, s=None):
            if m < MACROS:
                if not s:
                    ts[m] = work.tile([P, SUB, PACK, P], F32, name="t", bufs=3)
                nc.scalar.activation(
                    out=ts[m][:, rows(s)],
                    in_=xs[m][:, rows(s)].rearrange("r s (c t) -> r s t c", t=PACK),
                    func=ACT.Tanh,
                )

        def square(m, s=None):
            if m < MACROS:
                if not s:
                    t2s[m] = work.tile([P, SUB, PACK, P], F32, name="t2", bufs=3)
                nc.scalar.activation(out=t2s[m][:, rows(s)], in_=ts[m][:, rows(s)], func=ACT.Square)

        def make_g(m, s):
            if m < MACROS:
                if s == 0:
                    gs[m] = work.tile([P, SUB, PACK, P], F32, name="g")
                nc.vector.scalar_tensor_tensor(
                    out=gs[m][:, s],
                    in0=t2s[m][:, s],
                    scalar=-1.0,
                    in1=ks[m][:, s].rearrange("r (c t) -> r t c", t=PACK),
                    op0=ALU.add,
                    op1=ALU.mult,
                )

        def make_tj(m):
            if m < MACROS:
                tjs[m] = work.tile([P, SUB, PACK, P], F32, name="tj")
                for s in range(SUB):
                    nc.vector.scalar_tensor_tensor(
                        out=tjs[m][:, s],
                        in0=ts[m][:, s],
                        scalar=2.0,
                        in1=js[m][:, s].rearrange("r (c t) -> r t c", t=PACK),
                        op0=ALU.mult,
                        op1=ALU.mult,
                    )

        def make_b(m, s, pool=False):
            if m < MACROS:
                if m not in bt:
                    bt[m] = work.tile([P, SUB, PACK, P], F32, name="b_t")
                if pool:
                    nc.gpsimd.tensor_tensor(out=bt[m][:, s], in0=tjs[m][:, s], in1=gs[m][:, s], op=ALU.mult)
                else:
                    nc.vector.tensor_tensor(out=bt[m][:, s], in0=tjs[m][:, s], in1=gs[m][:, s], op=ALU.mult)

        def make_bs(m, q, pool=False):
            if m < MACROS:
                if pool:
                    bt[m] = work.tile([P, SUB, PACK, P], F32, name="b_t")
                cols = slice(q, N * PACK) if pool else slice(0, q)
                flat = "r s t c -> r (s t c)"
                args = dict(
                    out=bt[m][:].rearrange(flat)[:, cols],
                    in0=tjs[m][:].rearrange(flat)[:, cols],
                    in1=gs[m][:].rearrange(flat)[:, cols],
                    op=ALU.mult,
                )
                if pool:
                    nc.gpsimd.tensor_tensor(**args)
                else:
                    nc.vector.tensor_tensor(**args)

        def make_a(m, s):
            if s == 0:
                at[m] = work.tile([P, SUB, PACK, P], F32, name="a_t")
            nc.vector.scalar_tensor_tensor(
                out=at[m][:, s], in0=t2s[m][:, s], scalar=-1.0, in1=vb[m, s][:], op0=ALU.add, op1=ALU.mult
            )

        def turn_g(m, s):
            if m < MACROS:
                gb[m, s] = psum.tile([P, PACK, P], F32, name="bank_g%d" % s)
                for t in range(PACK):
                    nc.tensor.transpose(gb[m, s][:, t, :], gs[m][:, s, t, :], ident[:])

        def turn_u(m, s):
            ub[m, s] = psum.tile([P, PACK, P], F32, name="bank_u%d" % s)
            for t in range(PACK):
                for part, first in ((bt, True), (at, False)):
                    nc.tensor.matmul(
                        ub[m, s][:, t, :],
                        lhsT=part[m][:, s, t, :],
                        rhs=ident[:],
                        is_transpose=True,
                        start=first,
                        stop=not first,
                    )

        def copy_g(m, s):
            if m < MACROS:
                if s == 0:
                    gg[m] = work.tile([P, N, PACK], BF16, name="g_grp", align_bytes=64)
                nc.scalar.copy(out=gg[m][:, s * P : (s + 1) * P, :], in_=gb[m, s][:].rearrange("p t r -> p r t"))

        def copy_u(m, s, vector=False):
            if s == 0:
                ug[m] = work.tile([P, N, PACK], BF16, name="u_grp", align_bytes=64)
            dst = ug[m][:, s * P : (s + 1) * P, :]
            src = ub[m, s][:].rearrange("p t r -> p r t")
            if vector:
                nc.vector.tensor_copy(out=dst, in_=src)
            else:
                nc.scalar.copy(out=dst, in_=src)

        def quant(done, src, m, s, name):
            if not s:
                done[m] = (
                    work.tile([P, N], U32, name="codes_" + name, align_bytes=64),
                    work.tile([P, N], U8, name="scales_" + name, align_bytes=64),
                )
            codes, scales = done[m]
            cols = slice(0, N) if s is None else slice(s * P, (s + 1) * P)
            nc.vector.quantize_mx(
                out=codes[:, cols].bitcast(FP8X4),
                scales=scales[:, cols],
                in_=src[m][:, cols, :].rearrange("p n t -> p (n t)"),
            )

        def quant_g(m, s=None):
            if m < MACROS:
                quant(gq, gg, m, s, "g")

        def quant_u(m, s=None):
            if m >= 0:
                quant(uq, ug, m, s, "u")

        def mm(operand, w_codes, w_scales, bank, s):
            codes, scales = operand
            cols = slice(s * P, (s + 1) * P)
            nc.tensor.matmul_mx(
                out=bank,
                lhsT=codes[:, cols].bitcast(FP8X4),
                lhsT_scale=scales[:, cols],
                rhs=w_codes[:].bitcast(FP8X4),
                rhs_scale=w_scales[:],
                start=True,
                stop=True,
            )

        def mm_v(m, s):
            if m < MACROS:
                vb[m, s] = psum.tile([P, PACK, P], F32, name="bank_v%d" % s)
                mm(gq[m], wj_codes, wj_scales, vb[m, s][:].rearrange("r t c -> r (t c)"), s)

        def mm_o(m, s):
            if m >= 0:
                ob[m, s] = psum.tile([P, D], F32, name="bank_o%d" % s)
                mm(uq[m], wi_codes, wi_scales, ob[m, s][:], s)

        def copy_out(m, s, vector=False):
            if m >= 0:
                if s == 0:
                    outs[m] = work.tile([P, SUB, D], F32, name="o_t", bufs=3)
                if vector:
                    nc.vector.tensor_copy(out=outs[m][:, s], in_=ob[m, s][:])
                else:
                    nc.scalar.copy(out=outs[m][:, s], in_=ob[m, s][:])

        def store(m, s=None):
            if m >= 0:
                nc.sync.dma_start(out=o_h[m][:, rows(s)], in_=outs[m][:, rows(s)])

        def turn_w(src, half, bank):
            words = src[:].rearrange("m c k -> m (c k)").bitcast(F32).rearrange("m (c w) -> m c w", c=PACK)
            for u in range(2):
                for c in range(2):
                    nc.tensor.transpose(bank[:, u, c, :], words[:, 2 * half + c, u : D // 2 : 2], ident[:])

        wbank = {}

        def turn_wj(h):
            wbank["j", h] = psum.tile([P, 2, 2, P], F32, name="bank_o%d" % h)
            turn_w(wj_raw, h, wbank["j", h])

        def copy_wj(h, vector=True):
            dst = wj_grp[:, h * N : (h + 1) * N, :].rearrange("p n t -> p (n t)").bitcast(F32).rearrange("p (n u) -> p n u", u=2)
            src = wbank["j", h][:].rearrange("p u c m -> p (c m) u")
            if vector:
                nc.vector.tensor_copy(out=dst, in_=src)
            else:
                nc.scalar.copy(out=dst, in_=src)

        def widen(h, vector=True):
            dst, src = wi_val[:, 2 * h : 2 * h + 2], wi_byte[:, 2 * h : 2 * h + 2].bitcast(FP8)
            if vector:
                nc.vector.tensor_copy(out=dst, in_=src)
            else:
                nc.scalar.copy(out=dst, in_=src)

        def turn_wi(h):
            wbank["i", h] = psum.tile([P, 2, 2, P], F32, name="bank_o%d" % h)
            turn_w(wi_val, h, wbank["i", h])

        def scale_wi(h):
            nc.vector.tensor_tensor(
                out=wi_grp[:, h * N : (h + 1) * N, :].rearrange("p n (u e) -> p n u e", u=2),
                in0=wbank["i", h][:].rearrange("p u c m -> p (u c m)").bitcast(BF16).rearrange("p (u n e) -> p n u e", u=2, e=2),
                in1=wi_sc[:].rearrange("p (u e) -> p u e", u=2).unsqueeze(1).to_broadcast([P, N, 2, 2]),
                op=ALU.mult,
            )

        def quant_wj():
            quant_w(wj_codes, wj_scales, wj_grp)

        def quant_wi():
            quant_w(wi_codes, wi_scales, wi_grp)

        def load_wj():
            nc.sync.dma_start(out=wj_raw[:], in_=w_j.rearrange("(m t) k -> m t k", t=PACK))

        def load_wi():
            nc.sync.dma_start(out=wi_byte[:], in_=w_i_bytes.rearrange("(c m) k -> m c k", m=P))

        def load_sc():
            nc.sync.dma_start(out=wi_sc[:], in_=w_i_scale.rearrange("o (p t) -> p (o t)", t=PACK))

        def prepare():
            nc.vector.memset(zero[:], 0.0)
            nc.scalar.activation(out=warm[:], in_=zero[:], func=ACT.Tanh)
            make_identity(nc, ident[:])

        def quant_w(codes, scales, src):
            nc.vector.quantize_mx(
                out=codes[:].bitcast(FP8X4), scales=scales[:], in_=src[:].rearrange("p n t -> p (n t)")
            )
        BQ = 320
        load_x_half(0); load_x_half(1); load_wi(); load_k(0); load_wj(); load_j(0); load_sc(); load_x(1); load_k(1); load_j(1)
        for m in range(2, 5):
            load(m)
        prepare()
        for s in range(SUB):
            tanh(0, s)
        for s in range(SUB):
            square(0, s)
        for s in range(SUB):
            make_g(0, s)
        for h in range(2):
            turn_wj(h)
        widen(0, vector=False)
        copy_wj(0, vector=False)
        widen(1, vector=False)
        make_tj(0)
        for s in range(SUB):
            make_b(0, s, pool=True)
        copy_wj(1)
        for s in range(SUB):
            turn_g(0, s)
        quant_wj()
        for h in range(2):
            turn_wi(h)
        tanh(1)
        for s in range(SUB):
            copy_g(0, s)
        for h in range(2):
            scale_wi(h)
        quant_g(0)
        for s in range(SUB):
            mm_v(0, s)
        quant_wi()
        tanh(2)
        square(1)
        for m in range(MACROS):
            load(m + 5)
            tanh(m + 3)
            square(m + 2)
            make_tj(m + 1)
            quant_u(m - 1)
            for s in range(SUB):
                make_g(m + 1, s)
            for s in range(SUB):
                mm_o(m - 1, s)
            for s in range(SUB):
                turn_g(m + 1, s)
            make_bs(m + 1, BQ, pool=True)
            if m >= MACROS - 2:
                copy_out(m - 1, 0)
            for s in range(SUB):
                make_a(m, s)
                copy_g(m + 1, s)
            if m < MACROS - 2:
                copy_out(m - 1, 0)
            copy_out(m - 1, 1, vector=True)
            store(m - 1)
            make_bs(m + 1, BQ)
            for s in range(SUB):
                turn_u(m, s)
                copy_u(m, s)
            quant_g(m + 1)
            for s in range(SUB):
                mm_v(m + 1, s)
        for s in range(SUB):
            quant_u(MACROS - 1, s)
            mm_o(MACROS - 1, s)
            copy_out(MACROS - 1, s, vector=(s == 1))
            store(MACROS - 1, s)
